import numpy as np
import ml_dtypes


def mxq(x, axis, fmt="e4m3"):
    dtype, down = {"e4m3": (ml_dtypes.float8_e4m3fn, 7), "e5m2": (ml_dtypes.float8_e5m2, 14)}[fmt]
    v = np.moveaxis(np.asarray(x, np.float32).astype(ml_dtypes.bfloat16).astype(np.float64), axis, -1)
    blocks = v.reshape(v.shape[:-1] + (-1, 32))
    amax = np.abs(blocks).max(-1, keepdims=True)
    byte = np.maximum(np.where(amax > 0, np.frexp(amax)[1] - 1 + 127, 0) - down, 1)
    scale = np.exp2(byte - 127.0)
    codes = (blocks / scale).astype(np.float32).astype(dtype).astype(np.float64)
    return np.moveaxis((codes * scale).reshape(v.shape), -1, axis)


WIDE = False


def mx_kscale(k):
    if not WIDE:
        return np.ones(k)
    levels = np.array([20, -20, 10, -10, 0])
    a = np.random.permutation(np.resize(levels, k // 512 * 4)).reshape(k // 512, 4)
    idx = np.arange(k)
    return np.exp2(a[idx // 512, idx % 128 // 32])


BF16 = ml_dtypes.bfloat16


def bf(x):
    return np.asarray(x, np.float32).astype(BF16)


def f64(x):
    return np.asarray(x).astype(np.float64)


B, T, D, H = 4, 1024, 1024, 512
QMAX = 127


def _grid(shape, axis):
    a = np.random.randint(-QMAX, QMAX + 1, shape)
    one = list(shape)
    one[axis] = 1
    pos = np.random.randint(0, shape[axis], one)
    sgn = 2 * np.random.randint(0, 2, one) - 1
    np.put_along_axis(a, pos, QMAX * sgn, axis)
    return a


def setup_inputs():
    u = np.asarray(mx_kscale(H), np.float64)
    x = _grid((B, T, D), 2) * 2.0 ** -6
    w = _grid((D, H), 0) * 2.0 ** -6 / u
    g = np.random.standard_normal((B, T, H)) * np.exp2(np.random.randint(-12, 1, (B, T, 1))) * u
    return {"inputs": bf(x), "kernel": bf(w), "grad_out": bf(g)}


def reference(inputs, kernel, grad_out):
    return mxq(f64(grad_out), 2, "e5m2") @ mxq(f64(kernel), 1, "e4m3").T

@@ -1,0 +1,184 @@
+from contextlib import ExitStack
+
+import concourse.mybir as mybir
+from concourse.masks import make_identity
+
+F32 = mybir.dt.float32
+BF16 = mybir.dt.bfloat16
+U32 = mybir.dt.uint32
+U8 = mybir.dt.uint8
+E4M3X4 = mybir.dt.float8_e4m3fn_x4
+E5M2X4 = mybir.dt.float8_e5m2_x4
+
+P = 128
+H = 512
+D = 1024
+TOKENS = 4096
+J = TOKENS // P
+HW = H // 2
+BANK = 512
+GROUPS = (2, 2, 4, 4, 4, 4, 4, 4, 4)
+LOAD_TILES = (2, 2, 4, 8, 8, 8)
+STORE_TILES = (2, 2, 4, 4, 4, 4, 4, 4, 4)
+PINNED = True
+
+FLOPS = 2 * TOKENS * D * H
+BYTES = TOKENS * H * 2 + D * H * 2 + TOKENS * D * 4
+
+
+def tile_densegeneral_t_kernel(tc, inputs, kernel, grad_out, out):
+    nc = tc.nc
+    g_dram = grad_out.flatten_outer_dims().rearrange("(p j) h -> p (j h)", j=J)
+    o_dram = out.flatten_outer_dims().rearrange("(p j) d -> p (j d)", j=J)
+    w_dram = kernel.rearrange("(q p b) h -> p q (b h)", q=4, b=2)
+
+    with ExitStack() as stack:
+        if PINNED:
+            stack.enter_context(tc.manual_schedule())
+        keep = stack.enter_context(tc.tile_pool(name="keep", bufs=1))
+        ring = stack.enter_context(tc.tile_pool(name="ring", bufs=3))
+        psum = stack.enter_context(tc.psum_pool(name="psum", bufs=1))
+
+        w_half = []
+        g_where = []
+        g_loaded = [0]
+
+        def load_w(half):
+            w_sb = keep.tile([P, 4 * H], BF16, name="w_sb%d" % half)
+            nc.sync.dma_start(
+                out=w_sb[:].rearrange("p (q x) -> p q x", q=2), in_=w_dram[:, 2 * half : 2 * half + 2, :]
+            )
+            w_half.append(w_sb)
+
+        def load_g(count):
+            first = g_loaded[0]
+            g_sb = keep.tile([P, count * H], BF16, name="g_sb%d" % first)
+            nc.sync.dma_start(out=g_sb[:], in_=g_dram[:, first * H : (first + count) * H])
+            for local in range(count):
+                g_where.append((g_sb, local))
+            g_loaded[0] = first + count
+
+        load_w(0)
+        load_g(LOAD_TILES[0])
+        load_w(1)
+        for count in LOAD_TILES[1:]:
+            load_g(count)
+
+        ident = keep.tile([P, P], F32, name="ident")
+        make_identity(nc, ident[:])
+
+        w_grouped = keep.tile([P, 4 * D], BF16, name="w_grouped", align_bytes=64)
+        w_codes = keep.tile([P, D], U32, name="w_codes", align_bytes=64)
+        w_scales = keep.tile([P, D], U8, name="w_scales", align_bytes=64)
+
+        def transpose_w(half):
+            src = w_half[half][:].bitcast(F32)
+            for q in range(2):
+                bank = psum.tile([P, BANK], F32, name="tp", tag="tp", bufs=3)
+                for s in range(4):
+                    col = q * 2 * HW + s * P
+                    nc.tensor.transpose(out=bank[:, s * P : (s + 1) * P], in_=src[:, col : col + P], identity=ident[:])
+                quarter = 2 * half + q
+                dst = w_grouped[:].bitcast(F32)[:, quarter * BANK : (quarter + 1) * BANK]
+                dst = dst.rearrange("p (c b u) -> p c b u", b=2, u=2)
+                view = bank[:].rearrange("p (b u c) -> p c b u", b=2, u=2)
+                if q == 0:
+                    nc.vector.tensor_copy(out=dst, in_=view)
+                else:
+                    nc.scalar.copy(out=dst, in_=view)
+
+        def quantise_w(half):
+            nc.vector.quantize_mx(
+                out=w_codes[:, half * BANK : (half + 1) * BANK].bitcast(E4M3X4),
+                scales=w_scales[:, half * BANK : (half + 1) * BANK],
+                in_=w_grouped[:, half * 4 * BANK : (half + 1) * 4 * BANK],
+            )
+
+        group_first = [sum(GROUPS[:g]) for g in range(len(GROUPS))]
+        grouped_of = {}
+        codes_of = {}
+
+        def transpose_group(g):
+            tiles = GROUPS[g]
+            grouped = ring.tile([P, tiles * H], BF16, name="grouped", tag="grouped", align_bytes=64)
+            words = grouped[:].bitcast(F32)
+            for k in range(tiles // 2):
+                bank = psum.tile([P, BANK], F32, name="tp", tag="tp", bufs=3)
+                for s in range(4):
+                    g_sb, local = g_where[group_first[g] + 2 * k + s // 2]
+                    col = local * HW + (s % 2) * P
+                    nc.tensor.transpose(
+                        out=bank[:, s * P : (s + 1) * P],
+                        in_=g_sb[:].bitcast(F32)[:, col : col + P],
+                        identity=ident[:],
+                    )
+                dst = words[:, k * BANK : (k + 1) * BANK].rearrange("p (j r u) -> p j r u", j=2, u=2)
+                view = bank[:].rearrange("p (j u r) -> p j r u", j=2, u=2)
+                if k == 0:
+                    nc.vector.tensor_copy(out=dst, in_=view)
+                else:
+                    nc.scalar.copy(out=dst, in_=view)
+            grouped_of[g] = grouped
+
+        def quantise_group(g):
+            tiles = GROUPS[g]
+            codes = ring.tile([P, tiles * P], U32, name="g_codes", tag="g_codes", align_bytes=64)
+            scales = ring.tile([P, tiles * P], U8, name="g_scales", tag="g_scales", align_bytes=64)
+            nc.vector.quantize_mx(out=codes[:].bitcast(E5M2X4), scales=scales[:], in_=grouped_of[g][:])
+            codes_of[g] = (codes, scales)
+
+        o_where = []
+        o_tiles = []
+        first_tile = 0
+        for i, count in enumerate(STORE_TILES):
+            o_sb = keep.tile([P, count * D], F32, name="o_sb%d" % i)
+            o_tiles.append((o_sb, first_tile, count))
+            for local in range(count):
+                o_where.append((i, local))
+            first_tile += count
+        done = {}
+
+        def multiply(g, passes, on_vector):
+            codes, scales = codes_of[g]
+            for n, (t, half) in passes:
+                acc = psum.tile([P, BANK], F32, name="acc", tag="acc", bufs=5)
+                nc.tensor.matmul_mx(
+                    out=acc[:],
+                    lhsT=codes[:, t * P : (t + 1) * P].bitcast(E5M2X4),
+                    lhsT_scale=scales[:, t * P : (t + 1) * P],
+                    rhs=w_codes[:, half * BANK : (half + 1) * BANK].bitcast(E4M3X4),
+                    rhs_scale=w_scales[:, half * BANK : (half + 1) * BANK],
+                    start=True,
+                    stop=True,
+                )
+                i, local = o_where[group_first[g] + t]
+                o_sb, first, count = o_tiles[i]
+                dst = o_sb[:, local * D + half * BANK : local * D + (half + 1) * BANK]
+                if n in on_vector:
+                    nc.vector.tensor_copy(out=dst, in_=acc[:])
+                else:
+                    nc.scalar.copy(out=dst, in_=acc[:])
+                done[i] = done.get(i, 0) + 1
+                if done[i] == 2 * count:
+                    nc.sync.dma_start(out=o_dram[:, first * D : (first + count) * D], in_=o_sb[:])
+
+        transpose_w(0)
+        transpose_group(0)
+        quantise_w(0)
+        quantise_group(0)
+        transpose_w(1)
+        quantise_w(1)
+        for g in range(len(GROUPS)):
+            tiles = GROUPS[g]
+            if g == 0:
+                order = [(t, half) for half in range(2) for t in range(tiles)]
+            else:
+                order = [(t, half) for t in range(tiles) for half in range(2)]
+            order = list(enumerate(order))
+            on_vector = [n for n in range(1, 2 * tiles - 1, 2)]
+            if g + 1 < len(GROUPS):
+                transpose_group(g + 1)
+            multiply(g, order[:tiles], on_vector)
+            if g + 1 < len(GROUPS):
+                quantise_group(g + 1)
+            multiply(g, order[tiles:], on_vector)

@@ -19,7 +19,7 @@ HW = H // 2
 BANK = 512
 GROUPS = (2, 2, 4, 4, 4, 4, 4, 4, 4)
 LOAD_TILES = (2, 2, 4, 8, 8, 8)
-STORE_TILES = (2, 2, 4, 4, 4, 4, 4, 4, 4)
+STORE_TILES = (1, 1, 2, 2, 2, 4, 4, 4, 4, 4, 4)
 PINNED = True
 
 FLOPS = 2 * TOKENS * D * H
@@ -59,9 +59,8 @@ def tile_densegeneral_t_kernel(tc, inputs, kernel, grad_out, out):
             g_loaded[0] = first + count
 
         load_w(0)
-        load_g(LOAD_TILES[0])
         load_w(1)
-        for count in LOAD_TILES[1:]:
+        for count in LOAD_TILES:
             load_g(count)
 
         ident = keep.tile([P, P], F32, name="ident")
@@ -114,7 +113,7 @@ def tile_densegeneral_t_kernel(tc, inputs, kernel, grad_out, out):
                     )
                 dst = words[:, k * BANK : (k + 1) * BANK].rearrange("p (j r u) -> p j r u", j=2, u=2)
                 view = bank[:].rearrange("p (j u r) -> p j r u", j=2, u=2)
-                if k == 0:
+                if k == 0 and g > 0:
                     nc.vector.tensor_copy(out=dst, in_=view)
                 else:
                     nc.scalar.copy(out=dst, in_=view)
@@ -163,18 +162,14 @@ def tile_densegeneral_t_kernel(tc, inputs, kernel, grad_out, out):
                     nc.sync.dma_start(out=o_dram[:, first * D : (first + count) * D], in_=o_sb[:])
 
         transpose_w(0)
-        transpose_group(0)
         quantise_w(0)
-        quantise_group(0)
         transpose_w(1)
         quantise_w(1)
+        transpose_group(0)
+        quantise_group(0)
         for g in range(len(GROUPS)):
             tiles = GROUPS[g]
-            if g == 0:
-                order = [(t, half) for half in range(2) for t in range(tiles)]
-            else:
-                order = [(t, half) for t in range(tiles) for half in range(2)]
-            order = list(enumerate(order))
+            order = list(enumerate([(t, half) for t in range(tiles) for half in range(2)]))
             on_vector = [n for n in range(1, 2 * tiles - 1, 2)]
             if g + 1 < len(GROUPS):
                 transpose_group(g + 1)

@@ -18,8 +18,8 @@ J = TOKENS // P
 HW = H // 2
 BANK = 512
 GROUPS = (2, 2, 4, 4, 4, 4, 4, 4, 4)
-LOAD_TILES = (2, 2, 4, 8, 8, 8)
-STORE_TILES = (1, 1, 2, 2, 2, 4, 4, 4, 4, 4, 4)
+LOAD_TILES = (2, 2, 4, 8, 16)
+STORE_TILES = (2, 2, 4, 4, 4, 8, 8)
 PINNED = True
 
 FLOPS = 2 * TOKENS * D * H
@@ -170,7 +170,7 @@ def tile_densegeneral_t_kernel(tc, inputs, kernel, grad_out, out):
         for g in range(len(GROUPS)):
             tiles = GROUPS[g]
             order = list(enumerate([(t, half) for t in range(tiles) for half in range(2)]))
-            on_vector = [n for n in range(1, 2 * tiles - 1, 2)]
+            on_vector = [n for n in range(1, 2 * tiles - 1 + 2 * (g % 2), 2)]
             if g + 1 < len(GROUPS):
                 transpose_group(g + 1)
             multiply(g, order[:tiles], on_vector)

@@ -18,7 +18,7 @@ J = TOKENS // P
 HW = H // 2
 BANK = 512
 GROUPS = (2, 2, 4, 4, 4, 4, 4, 4, 4)
-LOAD_TILES = (2, 2, 4, 8, 16)
+LOAD_TILES = (4, 12, 16)
 STORE_TILES = (2, 2, 4, 4, 4, 8, 8)
 PINNED = True
 
@@ -30,7 +30,7 @@ def tile_densegeneral_t_kernel(tc, inputs, kernel, grad_out, out):
     nc = tc.nc
     g_dram = grad_out.flatten_outer_dims().rearrange("(p j) h -> p (j h)", j=J)
     o_dram = out.flatten_outer_dims().rearrange("(p j) d -> p (j d)", j=J)
-    w_dram = kernel.rearrange("(q p b) h -> p q (b h)", q=4, b=2)
+    w_dram = kernel.rearrange("(q p b) h -> p q (b h)", q=2, b=4)
 
     with ExitStack() as stack:
         if PINNED:
@@ -45,9 +45,7 @@ def tile_densegeneral_t_kernel(tc, inputs, kernel, grad_out, out):
 
         def load_w(half):
             w_sb = keep.tile([P, 4 * H], BF16, name="w_sb%d" % half)
-            nc.sync.dma_start(
-                out=w_sb[:].rearrange("p (q x) -> p q x", q=2), in_=w_dram[:, 2 * half : 2 * half + 2, :]
-            )
+            nc.sync.dma_start(out=w_sb[:], in_=w_dram[:, half, :])
             w_half.append(w_sb)
 
         def load_g(count):
@@ -77,11 +75,10 @@ def tile_densegeneral_t_kernel(tc, inputs, kernel, grad_out, out):
                 for s in range(4):
                     col = q * 2 * HW + s * P
                     nc.tensor.transpose(out=bank[:, s * P : (s + 1) * P], in_=src[:, col : col + P], identity=ident[:])
-                quarter = 2 * half + q
-                dst = w_grouped[:].bitcast(F32)[:, quarter * BANK : (quarter + 1) * BANK]
-                dst = dst.rearrange("p (c b u) -> p c b u", b=2, u=2)
+                dst = w_grouped[:].bitcast(F32)[:, half * 2 * BANK : (half + 1) * 2 * BANK]
+                dst = dst.rearrange("p (c b u) -> p c b u", b=4, u=2)[:, :, 2 * q : 2 * q + 2, :]
                 view = bank[:].rearrange("p (b u c) -> p c b u", b=2, u=2)
-                if q == 0:
+                if half == 0:
                     nc.vector.tensor_copy(out=dst, in_=view)
                 else:
                     nc.scalar.copy(out=dst, in_=view)

@@ -19,7 +19,7 @@ HW = H // 2
 BANK = 512
 GROUPS = (2, 2, 4, 4, 4, 4, 4, 4, 4)
 LOAD_TILES = (4, 12, 16)
-STORE_TILES = (2, 2, 4, 4, 4, 8, 8)
+STORE_TILES = (2, 2, 4, 4, 4, 4, 4, 4, 4)
 PINNED = True
 
 FLOPS = 2 * TOKENS * D * H

@@ -19,7 +19,7 @@ HW = H // 2
 BANK = 512
 GROUPS = (2, 2, 4, 4, 4, 4, 4, 4, 4)
 LOAD_TILES = (4, 12, 16)
-STORE_TILES = (2, 2, 4, 4, 4, 4, 4, 4, 4)
+STORE_TILES = (2, 2, 2, 2, 4, 4, 4, 4, 4, 4)
 PINNED = True
 
 FLOPS = 2 * TOKENS * D * H

@@ -21,6 +21,7 @@ GROUPS = (2, 2, 4, 4, 4, 4, 4, 4, 4)
 LOAD_TILES = (4, 12, 16)
 STORE_TILES = (2, 2, 2, 2, 4, 4, 4, 4, 4, 4)
 PINNED = True
+SCALAR_STORE_LAG = 3
 
 FLOPS = 2 * TOKENS * D * H
 BYTES = TOKENS * H * 2 + D * H * 2 + TOKENS * D * 4
@@ -133,10 +134,20 @@ def tile_densegeneral_t_kernel(tc, inputs, kernel, grad_out, out):
                 o_where.append((i, local))
             first_tile += count
         done = {}
+        waiting = []
+
+        def issue_waiting(everything):
+            for entry in list(waiting):
+                entry[0] -= 1
+                if everything or entry[0] <= 0:
+                    o_sb, first, count = o_tiles[entry[1]]
+                    nc.scalar.dma_start(out=o_dram[:, first * D : (first + count) * D], in_=o_sb[:])
+                    waiting.remove(entry)
 
         def multiply(g, passes, on_vector):
             codes, scales = codes_of[g]
             for n, (t, half) in passes:
+                issue_waiting(False)
                 acc = psum.tile([P, BANK], F32, name="acc", tag="acc", bufs=5)
                 nc.tensor.matmul_mx(
                     out=acc[:],
@@ -156,7 +167,10 @@ def tile_densegeneral_t_kernel(tc, inputs, kernel, grad_out, out):
                     nc.scalar.copy(out=dst, in_=acc[:])
                 done[i] = done.get(i, 0) + 1
                 if done[i] == 2 * count:
-                    nc.sync.dma_start(out=o_dram[:, first * D : (first + count) * D], in_=o_sb[:])
+                    if count < 4 or i % 2 == 0:
+                        nc.sync.dma_start(out=o_dram[:, first * D : (first + count) * D], in_=o_sb[:])
+                    else:
+                        waiting.append([SCALAR_STORE_LAG, i])
 
         transpose_w(0)
         quantise_w(0)
@@ -174,3 +188,4 @@ def tile_densegeneral_t_kernel(tc, inputs, kernel, grad_out, out):
             if g + 1 < len(GROUPS):
                 quantise_group(g + 1)
             multiply(g, order[tiles:], on_vector)
+        issue_waiting(True)

from contextlib import ExitStack

import concourse.mybir as mybir
from concourse.masks import make_identity

F32 = mybir.dt.float32
BF16 = mybir.dt.bfloat16
U32 = mybir.dt.uint32
U8 = mybir.dt.uint8
E4M3X4 = mybir.dt.float8_e4m3fn_x4
E5M2X4 = mybir.dt.float8_e5m2_x4

P = 128
H = 512
D = 1024
TOKENS = 4096
J = TOKENS // P
HW = H // 2
BANK = 512
GROUPS = (2, 2, 4, 4, 4, 4, 4, 4, 4)
LOAD_TILES = (4, 12, 16)
STORE_TILES = (2, 2, 2, 2, 4, 4, 4, 4, 4, 4)
PINNED = True
SCALAR_STORE_LAG = 3

FLOPS = 2 * TOKENS * D * H
BYTES = TOKENS * H * 2 + D * H * 2 + TOKENS * D * 4


def tile_densegeneral_t_kernel(tc, inputs, kernel, grad_out, out):
    nc = tc.nc
    g_dram = grad_out.flatten_outer_dims().rearrange("(p j) h -> p (j h)", j=J)
    o_dram = out.flatten_outer_dims().rearrange("(p j) d -> p (j d)", j=J)
    w_dram = kernel.rearrange("(q p b) h -> p q (b h)", q=2, b=4)

    with ExitStack() as stack:
        if PINNED:
            stack.enter_context(tc.manual_schedule())
        keep = stack.enter_context(tc.tile_pool(name="keep", bufs=1))
        ring = stack.enter_context(tc.tile_pool(name="ring", bufs=3))
        psum = stack.enter_context(tc.psum_pool(name="psum", bufs=1))

        w_half = []
        g_where = []
        g_loaded = [0]

        def load_w(half):
            w_sb = keep.tile([P, 4 * H], BF16, name="w_sb%d" % half)
            nc.sync.dma_start(out=w_sb[:], in_=w_dram[:, half, :])
            w_half.append(w_sb)

        def load_g(count):
            first = g_loaded[0]
            g_sb = keep.tile([P, count * H], BF16, name="g_sb%d" % first)
            nc.sync.dma_start(out=g_sb[:], in_=g_dram[:, first * H : (first + count) * H])
            for local in range(count):
                g_where.append((g_sb, local))
            g_loaded[0] = first + count

        load_w(0)
        load_w(1)
        for count in LOAD_TILES:
            load_g(count)

        ident = keep.tile([P, P], F32, name="ident")
        make_identity(nc, ident[:])

        w_grouped = keep.tile([P, 4 * D], BF16, name="w_grouped", align_bytes=64)
        w_codes = keep.tile([P, D], U32, name="w_codes", align_bytes=64)
        w_scales = keep.tile([P, D], U8, name="w_scales", align_bytes=64)

        def transpose_w(half):
            src = w_half[half][:].bitcast(F32)
            for q in range(2):
                bank = psum.tile([P, BANK], F32, name="tp", tag="tp", bufs=3)
                for s in range(4):
                    col = q * 2 * HW + s * P
                    nc.tensor.transpose(out=bank[:, s * P : (s + 1) * P], in_=src[:, col : col + P], identity=ident[:])
                dst = w_grouped[:].bitcast(F32)[:, half * 2 * BANK : (half + 1) * 2 * BANK]
                dst = dst.rearrange("p (c b u) -> p c b u", b=4, u=2)[:, :, 2 * q : 2 * q + 2, :]
                view = bank[:].rearrange("p (b u c) -> p c b u", b=2, u=2)
                if half == 0:
                    nc.vector.tensor_copy(out=dst, in_=view)
                else:
                    nc.scalar.copy(out=dst, in_=view)

        def quantise_w(half):
            nc.vector.quantize_mx(
                out=w_codes[:, half * BANK : (half + 1) * BANK].bitcast(E4M3X4),
                scales=w_scales[:, half * BANK : (half + 1) * BANK],
                in_=w_grouped[:, half * 4 * BANK : (half + 1) * 4 * BANK],
            )

        group_first = [sum(GROUPS[:g]) for g in range(len(GROUPS))]
        grouped_of = {}
        codes_of = {}

        def transpose_group(g):
            tiles = GROUPS[g]
            grouped = ring.tile([P, tiles * H], BF16, name="grouped", tag="grouped", align_bytes=64)
            words = grouped[:].bitcast(F32)
            for k in range(tiles // 2):
                bank = psum.tile([P, BANK], F32, name="tp", tag="tp", bufs=3)
                for s in range(4):
                    g_sb, local = g_where[group_first[g] + 2 * k + s // 2]
                    col = local * HW + (s % 2) * P
                    nc.tensor.transpose(
                        out=bank[:, s * P : (s + 1) * P],
                        in_=g_sb[:].bitcast(F32)[:, col : col + P],
                        identity=ident[:],
                    )
                dst = words[:, k * BANK : (k + 1) * BANK].rearrange("p (j r u) -> p j r u", j=2, u=2)
                view = bank[:].rearrange("p (j u r) -> p j r u", j=2, u=2)
                if k == 0 and g > 0:
                    nc.vector.tensor_copy(out=dst, in_=view)
                else:
                    nc.scalar.copy(out=dst, in_=view)
            grouped_of[g] = grouped

        def quantise_group(g):
            tiles = GROUPS[g]
            codes = ring.tile([P, tiles * P], U32, name="g_codes", tag="g_codes", align_bytes=64)
            scales = ring.tile([P, tiles * P], U8, name="g_scales", tag="g_scales", align_bytes=64)
            nc.vector.quantize_mx(out=codes[:].bitcast(E5M2X4), scales=scales[:], in_=grouped_of[g][:])
            codes_of[g] = (codes, scales)

        o_where = []
        o_tiles = []
        first_tile = 0
        for i, count in enumerate(STORE_TILES):
            o_sb = keep.tile([P, count * D], F32, name="o_sb%d" % i)
            o_tiles.append((o_sb, first_tile, count))
            for local in range(count):
                o_where.append((i, local))
            first_tile += count
        done = {}
        waiting = []

        def issue_waiting(everything):
            for entry in list(waiting):
                entry[0] -= 1
                if everything or entry[0] <= 0:
                    o_sb, first, count = o_tiles[entry[1]]
                    nc.scalar.dma_start(out=o_dram[:, first * D : (first + count) * D], in_=o_sb[:])
                    waiting.remove(entry)

        def multiply(g, passes, on_vector):
            codes, scales = codes_of[g]
            for n, (t, half) in passes:
                issue_waiting(False)
                acc = psum.tile([P, BANK], F32, name="acc", tag="acc", bufs=5)
                nc.tensor.matmul_mx(
                    out=acc[:],
                    lhsT=codes[:, t * P : (t + 1) * P].bitcast(E5M2X4),
                    lhsT_scale=scales[:, t * P : (t + 1) * P],
                    rhs=w_codes[:, half * BANK : (half + 1) * BANK].bitcast(E4M3X4),
                    rhs_scale=w_scales[:, half * BANK : (half + 1) * BANK],
                    start=True,
                    stop=True,
                )
                i, local = o_where[group_first[g] + t]
                o_sb, first, count = o_tiles[i]
                dst = o_sb[:, local * D + half * BANK : local * D + (half + 1) * BANK]
                if n in on_vector:
                    nc.vector.tensor_copy(out=dst, in_=acc[:])
                else:
                    nc.scalar.copy(out=dst, in_=acc[:])
                done[i] = done.get(i, 0) + 1
                if done[i] == 2 * count:
                    if count < 4 or i % 2 == 0:
                        nc.sync.dma_start(out=o_dram[:, first * D : (first + count) * D], in_=o_sb[:])
                    else:
                        waiting.append([SCALAR_STORE_LAG, i])

        transpose_w(0)
        quantise_w(0)
        transpose_w(1)
        quantise_w(1)
        transpose_group(0)
        quantise_group(0)
        for g in range(len(GROUPS)):
            tiles = GROUPS[g]
            order = list(enumerate([(t, half) for t in range(tiles) for half in range(2)]))
            on_vector = [n for n in range(1, 2 * tiles - 1 + 2 * (g % 2), 2)]
            if g + 1 < len(GROUPS):
                transpose_group(g + 1)
            multiply(g, order[:tiles], on_vector)
            if g + 1 < len(GROUPS):
                quantise_group(g + 1)
            multiply(g, order[tiles:], on_vector)
        issue_waiting(True)
